import numpy as np
import ml_dtypes

BF16 = ml_dtypes.bfloat16


def bf(x):
    return np.asarray(x, np.float32).astype(BF16)


def f32(x):
    return np.asarray(x, np.float32)


def f64(x):
    return np.asarray(x).astype(np.float64)


def striped(idx):
    return np.tile(idx.reshape(-1, 16).T, (8, 1))


D, H, GATES, S, N = 256, 256, 4, 4096, 512


def sigmoid(v):
    return 1.0 / (1.0 + np.exp(-v))


def setup_inputs():
    stdv = 1.0 / np.sqrt(H)
    return {
        "x": bf(np.random.standard_normal((D, N))),
        "h_prev": bf(np.random.standard_normal((H, N))),
        "c_prev": f32(np.random.standard_normal((H, N))),
        "w_ih": bf(np.random.uniform(-stdv, stdv, (D, GATES * H))),
        "w_hh": bf(np.random.uniform(-stdv, stdv, (H, GATES * H))),
        "b_ih": f32(0.2 * np.random.standard_normal((GATES * H, 1))),
        "b_hh": f32(0.2 * np.random.standard_normal((GATES * H, 1))),
        "base": f32(0.3 * np.random.standard_normal((H, S))),
        "offs": striped(np.random.permutation(S)[:N]),
    }


def reference(x, h_prev, c_prev, w_ih, w_hh, b_ih, b_hh, base, offs):
    idx = offs[:16].T.reshape(-1)
    z = f64(w_ih).T @ f64(x) + f64(b_ih) + f64(w_hh).T @ f64(h_prev) + f64(b_hh)
    zi, zf, zo, zc = z.reshape(GATES, H, N)
    cell = sigmoid(zf) * f64(c_prev) + sigmoid(zi) * np.tanh(zc)
    out = f64(base).copy()
    out[:, idx] = sigmoid(zo) * np.tanh(cell)
    return out

@@ -1,0 +1,92 @@
+import concourse.mybir as mybir
+from concourse.masks import make_identity
+
+BF16, F32, U16 = mybir.dt.bfloat16, mybir.dt.float32, mybir.dt.uint16
+SIGMOID, TANH = mybir.ActivationFunctionType.Sigmoid, mybir.ActivationFunctionType.Tanh
+MULT, ADD = mybir.AluOpType.mult, mybir.AluOpType.add
+
+P = 128
+D = 256
+H = 256
+N = 512
+S = 4096
+K_STEPS = D // P
+H_BLOCKS = H // P
+GATE_I, GATE_F, GATE_O, GATE_CAND = 0, 1, 2, 3
+Z_BLOCKS = 4 * H_BLOCKS
+
+FLOPS = 2 * (D + H) * 4 * H * N
+
+
+def tile_share_lstm_cell_kernel(tc, x, h_prev, c_prev, w_ih, w_hh, b_ih, b_hh, base, offs, out):
+    nc = tc.nc
+    with (
+        tc.tile_pool(name="held", bufs=1) as held,
+        tc.tile_pool(name="work", bufs=2) as work,
+        tc.psum_pool(name="z_banks", bufs=6) as z_banks,
+        tc.psum_pool(name="bias_bank", bufs=1) as bias_bank,
+    ):
+        offsets = held.tile([P, N // 16], U16, name="offsets")
+        nc.sync.dma_start(offsets[:], offs)
+
+        b_ih_rows = held.tile([Z_BLOCKS, P], F32, name="b_ih_rows")
+        b_hh_rows = held.tile([Z_BLOCKS, P], F32, name="b_hh_rows")
+        nc.sync.dma_start(b_ih_rows[:], b_ih.rearrange("(g p) o -> g (p o)", p=P))
+        nc.sync.dma_start(b_hh_rows[:], b_hh.rearrange("(g p) o -> g (p o)", p=P))
+
+        x_sb = held.tile([P, K_STEPS, N], BF16, name="x_sb")
+        w_ih_sb = held.tile([P, K_STEPS, 4 * H], BF16, name="w_ih_sb")
+        h_sb = held.tile([P, K_STEPS, N], BF16, name="h_sb")
+        w_hh_sb = held.tile([P, K_STEPS, 4 * H], BF16, name="w_hh_sb")
+        nc.sync.dma_start(x_sb[:], x.rearrange("(p k) n -> p k n", k=K_STEPS))
+        nc.sync.dma_start(w_ih_sb[:], w_ih.rearrange("(p k) m -> p k m", k=K_STEPS))
+        nc.sync.dma_start(h_sb[:], h_prev.rearrange("(p k) n -> p k n", k=K_STEPS))
+        nc.sync.dma_start(w_hh_sb[:], w_hh.rearrange("(p k) m -> p k m", k=K_STEPS))
+
+        c_sb = [held.tile([P, N], F32, name=f"c_sb{blk}") for blk in range(H_BLOCKS)]
+        for blk in range(H_BLOCKS):
+            nc.sync.dma_start(c_sb[blk][:], c_prev[blk * P : (blk + 1) * P, :])
+
+        windows = [held.tile([P, S], F32, name=f"window{blk}") for blk in range(H_BLOCKS)]
+        for blk in range(H_BLOCKS):
+            nc.sync.dma_start(windows[blk][:], base[blk * P : (blk + 1) * P, :])
+
+        identity = held.tile([Z_BLOCKS, Z_BLOCKS], F32, name="identity")
+        make_identity(nc, identity[:])
+        bias_ps = bias_bank.tile([P, Z_BLOCKS], F32, name="bias_ps")
+        nc.tensor.matmul(bias_ps[:], b_ih_rows[:], identity[:], start=True, stop=False)
+        nc.tensor.matmul(bias_ps[:], b_hh_rows[:], identity[:], start=False, stop=True)
+        bias = held.tile([P, Z_BLOCKS], F32, name="bias")
+        nc.vector.tensor_copy(bias[:], bias_ps[:])
+
+        steps = [(w_ih_sb, x_sb, k) for k in range(K_STEPS)] + [(w_hh_sb, h_sb, k) for k in range(K_STEPS)]
+
+        for blk in range(H_BLOCKS):
+            gates = {}
+            for gate in (GATE_I, GATE_CAND, GATE_F, GATE_O):
+                g = gate * H_BLOCKS + blk
+                z = z_banks.tile([P, N], F32, name="z")
+                for step, (weights, moving, k) in enumerate(steps):
+                    nc.tensor.matmul(
+                        z[:],
+                        weights[:, k, g * P : (g + 1) * P],
+                        moving[:, k, :],
+                        start=(step == 0),
+                        stop=(step == len(steps) - 1),
+                    )
+                gates[gate] = work.tile([P, N], F32, name=f"gate{gate}")
+                nc.scalar.activation(
+                    gates[gate][:], z[:], TANH if gate == GATE_CAND else SIGMOID, bias=bias[:, g : g + 1]
+                )
+
+            written = work.tile([P, N], F32, name="written")
+            nc.vector.tensor_tensor(written[:], gates[GATE_I][:], gates[GATE_CAND][:], MULT)
+            kept = work.tile([P, N], F32, name="kept")
+            nc.vector.tensor_tensor(kept[:], gates[GATE_F][:], c_sb[blk][:], MULT)
+            cell = work.tile([P, N], F32, name="cell")
+            nc.vector.tensor_tensor(cell[:], kept[:], written[:], ADD)
+            tanh_cell = work.tile([P, N], F32, name="tanh_cell")
+            nc.scalar.activation(tanh_cell[:], cell[:], TANH)
+
+            nc.vector.tensor_tensor(windows[blk][:].indirect(offsets[:]), gates[GATE_O][:], tanh_cell[:], MULT)
+            nc.sync.dma_start(out[blk * P : (blk + 1) * P, :], windows[blk][:])

@@ -14,6 +14,7 @@ K_STEPS = D // P
 H_BLOCKS = H // P
 GATE_I, GATE_F, GATE_O, GATE_CAND = 0, 1, 2, 3
 Z_BLOCKS = 4 * H_BLOCKS
+WARM_MATMULS = 6
 
 FLOPS = 2 * (D + H) * 4 * H * N
 
@@ -25,7 +26,14 @@ def tile_share_lstm_cell_kernel(tc, x, h_prev, c_prev, w_ih, w_hh, b_ih, b_hh, b
         tc.tile_pool(name="work", bufs=2) as work,
         tc.psum_pool(name="z_banks", bufs=6) as z_banks,
         tc.psum_pool(name="bias_bank", bufs=1) as bias_bank,
+        tc.psum_pool(name="warm_bank", bufs=1) as warm_bank,
     ):
+        zeros = held.tile([P, N], BF16, name="zeros")
+        nc.vector.memset(zeros[:], 0.0)
+        warm_ps = warm_bank.tile([P, N], F32, name="warm_ps")
+        for repeat in range(WARM_MATMULS):
+            nc.tensor.matmul(warm_ps[:], zeros[:, :P], zeros[:], start=True, stop=True)
+
         offsets = held.tile([P, N // 16], U16, name="offsets")
         nc.sync.dma_start(offsets[:], offs)
 
@@ -44,11 +52,9 @@ def tile_share_lstm_cell_kernel(tc, x, h_prev, c_prev, w_ih, w_hh, b_ih, b_hh, b
         nc.sync.dma_start(w_hh_sb[:], w_hh.rearrange("(p k) m -> p k m", k=K_STEPS))
 
         c_sb = [held.tile([P, N], F32, name=f"c_sb{blk}") for blk in range(H_BLOCKS)]
-        for blk in range(H_BLOCKS):
-            nc.sync.dma_start(c_sb[blk][:], c_prev[blk * P : (blk + 1) * P, :])
-
         windows = [held.tile([P, S], F32, name=f"window{blk}") for blk in range(H_BLOCKS)]
         for blk in range(H_BLOCKS):
+            nc.sync.dma_start(c_sb[blk][:], c_prev[blk * P : (blk + 1) * P, :])
             nc.sync.dma_start(windows[blk][:], base[blk * P : (blk + 1) * P, :])
 
         identity = held.tile([Z_BLOCKS, Z_BLOCKS], F32, name="identity")
@@ -61,32 +67,37 @@ def tile_share_lstm_cell_kernel(tc, x, h_prev, c_prev, w_ih, w_hh, b_ih, b_hh, b
 
         steps = [(w_ih_sb, x_sb, k) for k in range(K_STEPS)] + [(w_hh_sb, h_sb, k) for k in range(K_STEPS)]
 
-        for blk in range(H_BLOCKS):
-            gates = {}
-            for gate in (GATE_I, GATE_CAND, GATE_F, GATE_O):
-                g = gate * H_BLOCKS + blk
-                z = z_banks.tile([P, N], F32, name="z")
-                for step, (weights, moving, k) in enumerate(steps):
-                    nc.tensor.matmul(
-                        z[:],
-                        weights[:, k, g * P : (g + 1) * P],
-                        moving[:, k, :],
-                        start=(step == 0),
-                        stop=(step == len(steps) - 1),
-                    )
-                gates[gate] = work.tile([P, N], F32, name=f"gate{gate}")
-                nc.scalar.activation(
-                    gates[gate][:], z[:], TANH if gate == GATE_CAND else SIGMOID, bias=bias[:, g : g + 1]
+        def gate_of(gate, blk):
+            g = gate * H_BLOCKS + blk
+            z = z_banks.tile([P, N], F32, name="z")
+            for step, (weights, moving, k) in enumerate(steps):
+                nc.tensor.matmul(
+                    z[:],
+                    weights[:, k, g * P : (g + 1) * P],
+                    moving[:, k, :],
+                    start=(step == 0),
+                    stop=(step == len(steps) - 1),
                 )
+            out_tile = work.tile([P, N], F32, name=f"gate{gate}")
+            nc.scalar.activation(out_tile[:], z[:], TANH if gate == GATE_CAND else SIGMOID, bias=bias[:, g : g + 1])
+            return out_tile
 
+        tanh_cells = []
+        for blk in range(H_BLOCKS):
+            gate_i = gate_of(GATE_I, blk)
+            gate_cand = gate_of(GATE_CAND, blk)
             written = work.tile([P, N], F32, name="written")
-            nc.vector.tensor_tensor(written[:], gates[GATE_I][:], gates[GATE_CAND][:], MULT)
+            nc.vector.tensor_tensor(written[:], gate_i[:], gate_cand[:], MULT)
+            gate_f = gate_of(GATE_F, blk)
             kept = work.tile([P, N], F32, name="kept")
-            nc.vector.tensor_tensor(kept[:], gates[GATE_F][:], c_sb[blk][:], MULT)
+            nc.vector.tensor_tensor(kept[:], gate_f[:], c_sb[blk][:], MULT)
             cell = work.tile([P, N], F32, name="cell")
             nc.vector.tensor_tensor(cell[:], kept[:], written[:], ADD)
             tanh_cell = work.tile([P, N], F32, name="tanh_cell")
             nc.scalar.activation(tanh_cell[:], cell[:], TANH)
+            tanh_cells.append(tanh_cell)
 
-            nc.vector.tensor_tensor(windows[blk][:].indirect(offsets[:]), gates[GATE_O][:], tanh_cell[:], MULT)
+        for blk in range(H_BLOCKS):
+            gate_o = gate_of(GATE_O, blk)
+            nc.vector.tensor_tensor(windows[blk][:].indirect(offsets[:]), gate_o[:], tanh_cells[blk][:], MULT)
             nc.sync.dma_start(out[blk * P : (blk + 1) * P, :], windows[blk][:])

@@ -67,37 +67,33 @@ def tile_share_lstm_cell_kernel(tc, x, h_prev, c_prev, w_ih, w_hh, b_ih, b_hh, b
 
         steps = [(w_ih_sb, x_sb, k) for k in range(K_STEPS)] + [(w_hh_sb, h_sb, k) for k in range(K_STEPS)]
 
-        def gate_of(gate, blk):
-            g = gate * H_BLOCKS + blk
-            z = z_banks.tile([P, N], F32, name="z")
-            for step, (weights, moving, k) in enumerate(steps):
-                nc.tensor.matmul(
-                    z[:],
-                    weights[:, k, g * P : (g + 1) * P],
-                    moving[:, k, :],
-                    start=(step == 0),
-                    stop=(step == len(steps) - 1),
-                )
-            out_tile = work.tile([P, N], F32, name=f"gate{gate}")
-            nc.scalar.activation(out_tile[:], z[:], TANH if gate == GATE_CAND else SIGMOID, bias=bias[:, g : g + 1])
-            return out_tile
-
-        tanh_cells = []
         for blk in range(H_BLOCKS):
-            gate_i = gate_of(GATE_I, blk)
-            gate_cand = gate_of(GATE_CAND, blk)
+            gates = {}
+            for gate in (GATE_I, GATE_CAND, GATE_F, GATE_O):
+                g = gate * H_BLOCKS + blk
+                z = z_banks.tile([P, N], F32, name="z")
+                for step, (weights, moving, k) in enumerate(steps):
+                    nc.tensor.matmul(
+                        z[:],
+                        weights[:, k, g * P : (g + 1) * P],
+                        moving[:, k, :],
+                        start=(step == 0),
+                        stop=(step == len(steps) - 1),
+                    )
+                gates[gate] = work.tile([P, N], F32, name=f"gate{gate}")
+                nc.scalar.activation(
+                    gates[gate][:], z[:], TANH if gate == GATE_CAND else SIGMOID, bias=bias[:, g : g + 1]
+                )
+
+            product_engine = nc.vector if blk == 0 else nc.gpsimd
             written = work.tile([P, N], F32, name="written")
-            nc.vector.tensor_tensor(written[:], gate_i[:], gate_cand[:], MULT)
-            gate_f = gate_of(GATE_F, blk)
+            product_engine.tensor_tensor(written[:], gates[GATE_I][:], gates[GATE_CAND][:], MULT)
             kept = work.tile([P, N], F32, name="kept")
-            nc.vector.tensor_tensor(kept[:], gate_f[:], c_sb[blk][:], MULT)
+            product_engine.tensor_tensor(kept[:], gates[GATE_F][:], c_sb[blk][:], MULT)
             cell = work.tile([P, N], F32, name="cell")
             nc.vector.tensor_tensor(cell[:], kept[:], written[:], ADD)
             tanh_cell = work.tile([P, N], F32, name="tanh_cell")
             nc.scalar.activation(tanh_cell[:], cell[:], TANH)
-            tanh_cells.append(tanh_cell)
 
-        for blk in range(H_BLOCKS):
-            gate_o = gate_of(GATE_O, blk)
-            nc.vector.tensor_tensor(windows[blk][:].indirect(offsets[:]), gate_o[:], tanh_cells[blk][:], MULT)
+            nc.vector.tensor_tensor(windows[blk][:].indirect(offsets[:]), gates[GATE_O][:], tanh_cell[:], MULT)
             nc.sync.dma_start(out[blk * P : (blk + 1) * P, :], windows[blk][:])

@@ -1,5 +1,4 @@
 import concourse.mybir as mybir
-from concourse.masks import make_identity
 
 BF16, F32, U16 = mybir.dt.bfloat16, mybir.dt.float32, mybir.dt.uint16
 SIGMOID, TANH = mybir.ActivationFunctionType.Sigmoid, mybir.ActivationFunctionType.Tanh
@@ -11,12 +10,12 @@ H = 256
 N = 512
 S = 4096
 K_STEPS = D // P
-H_BLOCKS = H // P
+HALVES = H // P
+GATES = 4
 GATE_I, GATE_F, GATE_O, GATE_CAND = 0, 1, 2, 3
-Z_BLOCKS = 4 * H_BLOCKS
 WARM_MATMULS = 6
 
-FLOPS = 2 * (D + H) * 4 * H * N
+FLOPS = 2 * (D + H) * GATES * H * N
 
 
 def tile_share_lstm_cell_kernel(tc, x, h_prev, c_prev, w_ih, w_hh, b_ih, b_hh, base, offs, out):
@@ -25,7 +24,6 @@ def tile_share_lstm_cell_kernel(tc, x, h_prev, c_prev, w_ih, w_hh, b_ih, b_hh, b
         tc.tile_pool(name="held", bufs=1) as held,
         tc.tile_pool(name="work", bufs=2) as work,
         tc.psum_pool(name="z_banks", bufs=6) as z_banks,
-        tc.psum_pool(name="bias_bank", bufs=1) as bias_bank,
         tc.psum_pool(name="warm_bank", bufs=1) as warm_bank,
     ):
         zeros = held.tile([P, N], BF16, name="zeros")
@@ -34,66 +32,72 @@ def tile_share_lstm_cell_kernel(tc, x, h_prev, c_prev, w_ih, w_hh, b_ih, b_hh, b
         for repeat in range(WARM_MATMULS):
             nc.tensor.matmul(warm_ps[:], zeros[:, :P], zeros[:], start=True, stop=True)
 
-        offsets = held.tile([P, N // 16], U16, name="offsets")
-        nc.sync.dma_start(offsets[:], offs)
-
-        b_ih_rows = held.tile([Z_BLOCKS, P], F32, name="b_ih_rows")
-        b_hh_rows = held.tile([Z_BLOCKS, P], F32, name="b_hh_rows")
-        nc.sync.dma_start(b_ih_rows[:], b_ih.rearrange("(g p) o -> g (p o)", p=P))
-        nc.sync.dma_start(b_hh_rows[:], b_hh.rearrange("(g p) o -> g (p o)", p=P))
+        table_warm = held.tile([P, 1], F32, name="table_warm")
+        nc.scalar.activation(table_warm[:], zeros[:, 0:1], SIGMOID)
 
         x_sb = held.tile([P, K_STEPS, N], BF16, name="x_sb")
-        w_ih_sb = held.tile([P, K_STEPS, 4 * H], BF16, name="w_ih_sb")
+        w_ih_sb = held.tile([P, K_STEPS, GATES * H], BF16, name="w_ih_sb")
         h_sb = held.tile([P, K_STEPS, N], BF16, name="h_sb")
-        w_hh_sb = held.tile([P, K_STEPS, 4 * H], BF16, name="w_hh_sb")
+        w_hh_sb = held.tile([P, K_STEPS, GATES * H], BF16, name="w_hh_sb")
         nc.sync.dma_start(x_sb[:], x.rearrange("(p k) n -> p k n", k=K_STEPS))
         nc.sync.dma_start(w_ih_sb[:], w_ih.rearrange("(p k) m -> p k m", k=K_STEPS))
         nc.sync.dma_start(h_sb[:], h_prev.rearrange("(p k) n -> p k n", k=K_STEPS))
         nc.sync.dma_start(w_hh_sb[:], w_hh.rearrange("(p k) m -> p k m", k=K_STEPS))
 
-        c_sb = [held.tile([P, N], F32, name=f"c_sb{blk}") for blk in range(H_BLOCKS)]
-        windows = [held.tile([P, S], F32, name=f"window{blk}") for blk in range(H_BLOCKS)]
-        for blk in range(H_BLOCKS):
-            nc.sync.dma_start(c_sb[blk][:], c_prev[blk * P : (blk + 1) * P, :])
-            nc.sync.dma_start(windows[blk][:], base[blk * P : (blk + 1) * P, :])
+        b_ih_sb = held.tile([P, GATES, HALVES], F32, name="b_ih_sb")
+        b_hh_sb = held.tile([P, GATES, HALVES], F32, name="b_hh_sb")
+        nc.sync.dma_start(b_ih_sb[:], b_ih.rearrange("(g p half) o -> p g (half o)", g=GATES, half=HALVES))
+        nc.sync.dma_start(b_hh_sb[:], b_hh.rearrange("(g p half) o -> p g (half o)", g=GATES, half=HALVES))
 
-        identity = held.tile([Z_BLOCKS, Z_BLOCKS], F32, name="identity")
-        make_identity(nc, identity[:])
-        bias_ps = bias_bank.tile([P, Z_BLOCKS], F32, name="bias_ps")
-        nc.tensor.matmul(bias_ps[:], b_ih_rows[:], identity[:], start=True, stop=False)
-        nc.tensor.matmul(bias_ps[:], b_hh_rows[:], identity[:], start=False, stop=True)
-        bias = held.tile([P, Z_BLOCKS], F32, name="bias")
-        nc.vector.tensor_copy(bias[:], bias_ps[:])
+        offsets = held.tile([P, N // 16], U16, name="offsets")
+        nc.sync.dma_start(offsets[:], offs)
+
+        c_sb = held.tile([P, HALVES, N], F32, name="c_sb")
+        nc.sync.dma_start(c_sb[:], c_prev.rearrange("(p half) n -> p half n", half=HALVES))
+
+        base_halves = base.rearrange("(p half) s -> half p s", half=HALVES)
+        out_halves = out.rearrange("(p half) s -> half p s", half=HALVES)
+        windows = [held.tile([P, S], F32, name=f"window{half}") for half in range(HALVES)]
+        for half in range(HALVES):
+            nc.sync.dma_start(windows[half][:], base_halves[half])
+
+        bias = held.tile([P, GATES, HALVES], F32, name="bias")
+        nc.vector.tensor_tensor(bias[:], b_ih_sb[:], b_hh_sb[:], ADD)
 
         steps = [(w_ih_sb, x_sb, k) for k in range(K_STEPS)] + [(w_hh_sb, h_sb, k) for k in range(K_STEPS)]
 
-        for blk in range(H_BLOCKS):
-            gates = {}
-            for gate in (GATE_I, GATE_CAND, GATE_F, GATE_O):
-                g = gate * H_BLOCKS + blk
-                z = z_banks.tile([P, N], F32, name="z")
-                for step, (weights, moving, k) in enumerate(steps):
-                    nc.tensor.matmul(
-                        z[:],
-                        weights[:, k, g * P : (g + 1) * P],
-                        moving[:, k, :],
-                        start=(step == 0),
-                        stop=(step == len(steps) - 1),
-                    )
-                gates[gate] = work.tile([P, N], F32, name=f"gate{gate}")
-                nc.scalar.activation(
-                    gates[gate][:], z[:], TANH if gate == GATE_CAND else SIGMOID, bias=bias[:, g : g + 1]
+        def gate_of(gate, half):
+            z = z_banks.tile([P, N], F32, name="z")
+            for step, (weights, moving, k) in enumerate(steps):
+                nc.tensor.matmul(
+                    z[:],
+                    weights[:, k, gate * H + half : (gate + 1) * H : HALVES],
+                    moving[:, k, :],
+                    start=(step == 0),
+                    stop=(step == len(steps) - 1),
                 )
+            gate_tile = work.tile([P, N], F32, name=f"gate{gate}")
+            nc.scalar.activation(
+                gate_tile[:], z[:], TANH if gate == GATE_CAND else SIGMOID, bias=bias[:, gate, half : half + 1]
+            )
+            return gate_tile
 
-            product_engine = nc.vector if blk == 0 else nc.gpsimd
+        tanh_cells = []
+        for half in range(HALVES):
+            gate_i = gate_of(GATE_I, half)
+            gate_cand = gate_of(GATE_CAND, half)
             written = work.tile([P, N], F32, name="written")
-            product_engine.tensor_tensor(written[:], gates[GATE_I][:], gates[GATE_CAND][:], MULT)
+            nc.vector.tensor_tensor(written[:], gate_i[:], gate_cand[:], MULT)
+            gate_f = gate_of(GATE_F, half)
             kept = work.tile([P, N], F32, name="kept")
-            product_engine.tensor_tensor(kept[:], gates[GATE_F][:], c_sb[blk][:], MULT)
+            nc.vector.tensor_tensor(kept[:], gate_f[:], c_sb[:, half, :], MULT)
             cell = work.tile([P, N], F32, name="cell")
             nc.vector.tensor_tensor(cell[:], kept[:], written[:], ADD)
             tanh_cell = work.tile([P, N], F32, name="tanh_cell")
             nc.scalar.activation(tanh_cell[:], cell[:], TANH)
+            tanh_cells.append(tanh_cell)
 
-            nc.vector.tensor_tensor(windows[blk][:].indirect(offsets[:]), gates[GATE_O][:], tanh_cell[:], MULT)
-            nc.sync.dma_start(out[blk * P : (blk + 1) * P, :], windows[blk][:])
+        for half in range(HALVES):
+            gate_o = gate_of(GATE_O, half)
+            nc.vector.tensor_tensor(windows[half][:].indirect(offsets[:]), gate_o[:], tanh_cells[half][:], MULT)
+            nc.sync.dma_start(out_halves[half], windows[half][:])

@@ -82,22 +82,19 @@ def tile_share_lstm_cell_kernel(tc, x, h_prev, c_prev, w_ih, w_hh, b_ih, b_hh, b
             )
             return gate_tile
 
-        tanh_cells = []
         for half in range(HALVES):
+            cell_engine = nc.vector if half == 0 else nc.gpsimd
             gate_i = gate_of(GATE_I, half)
             gate_cand = gate_of(GATE_CAND, half)
             written = work.tile([P, N], F32, name="written")
-            nc.vector.tensor_tensor(written[:], gate_i[:], gate_cand[:], MULT)
+            cell_engine.tensor_tensor(written[:], gate_i[:], gate_cand[:], MULT)
             gate_f = gate_of(GATE_F, half)
             kept = work.tile([P, N], F32, name="kept")
-            nc.vector.tensor_tensor(kept[:], gate_f[:], c_sb[:, half, :], MULT)
+            cell_engine.tensor_tensor(kept[:], gate_f[:], c_sb[:, half, :], MULT)
             cell = work.tile([P, N], F32, name="cell")
-            nc.vector.tensor_tensor(cell[:], kept[:], written[:], ADD)
+            cell_engine.tensor_tensor(cell[:], kept[:], written[:], ADD)
             tanh_cell = work.tile([P, N], F32, name="tanh_cell")
             nc.scalar.activation(tanh_cell[:], cell[:], TANH)
-            tanh_cells.append(tanh_cell)
-
-        for half in range(HALVES):
             gate_o = gate_of(GATE_O, half)
-            nc.vector.tensor_tensor(windows[half][:].indirect(offsets[:]), gate_o[:], tanh_cells[half][:], MULT)
+            nc.vector.tensor_tensor(windows[half][:].indirect(offsets[:]), gate_o[:], tanh_cell[:], MULT)
             nc.sync.dma_start(out_halves[half], windows[half][:])

@@ -13,7 +13,7 @@ K_STEPS = D // P
 HALVES = H // P
 GATES = 4
 GATE_I, GATE_F, GATE_O, GATE_CAND = 0, 1, 2, 3
-WARM_MATMULS = 6
+WARM_MATMULS = 4
 
 FLOPS = 2 * (D + H) * GATES * H * N
 
@@ -82,19 +82,22 @@ def tile_share_lstm_cell_kernel(tc, x, h_prev, c_prev, w_ih, w_hh, b_ih, b_hh, b
             )
             return gate_tile
 
+        tanh_cells = []
         for half in range(HALVES):
-            cell_engine = nc.vector if half == 0 else nc.gpsimd
             gate_i = gate_of(GATE_I, half)
             gate_cand = gate_of(GATE_CAND, half)
             written = work.tile([P, N], F32, name="written")
-            cell_engine.tensor_tensor(written[:], gate_i[:], gate_cand[:], MULT)
+            nc.vector.tensor_tensor(written[:], gate_i[:], gate_cand[:], MULT)
             gate_f = gate_of(GATE_F, half)
             kept = work.tile([P, N], F32, name="kept")
-            cell_engine.tensor_tensor(kept[:], gate_f[:], c_sb[:, half, :], MULT)
+            nc.vector.tensor_tensor(kept[:], gate_f[:], c_sb[:, half, :], MULT)
             cell = work.tile([P, N], F32, name="cell")
-            cell_engine.tensor_tensor(cell[:], kept[:], written[:], ADD)
+            nc.vector.tensor_tensor(cell[:], kept[:], written[:], ADD)
             tanh_cell = work.tile([P, N], F32, name="tanh_cell")
             nc.scalar.activation(tanh_cell[:], cell[:], TANH)
+            tanh_cells.append(tanh_cell)
+
+        for half in range(HALVES):
             gate_o = gate_of(GATE_O, half)
-            nc.vector.tensor_tensor(windows[half][:].indirect(offsets[:]), gate_o[:], tanh_cell[:], MULT)
+            nc.vector.tensor_tensor(windows[half][:].indirect(offsets[:]), gate_o[:], tanh_cells[half][:], MULT)
             nc.sync.dma_start(out_halves[half], windows[half][:])

@@ -46,8 +46,8 @@ def tile_share_lstm_cell_kernel(tc, x, h_prev, c_prev, w_ih, w_hh, b_ih, b_hh, b
 
         b_ih_sb = held.tile([P, GATES, HALVES], F32, name="b_ih_sb")
         b_hh_sb = held.tile([P, GATES, HALVES], F32, name="b_hh_sb")
-        nc.sync.dma_start(b_ih_sb[:], b_ih.rearrange("(g p half) o -> p g (half o)", g=GATES, half=HALVES))
-        nc.sync.dma_start(b_hh_sb[:], b_hh.rearrange("(g p half) o -> p g (half o)", g=GATES, half=HALVES))
+        nc.scalar.dma_start(b_ih_sb[:], b_ih.rearrange("(g p half) o -> p g (half o)", g=GATES, half=HALVES))
+        nc.scalar.dma_start(b_hh_sb[:], b_hh.rearrange("(g p half) o -> p g (half o)", g=GATES, half=HALVES))
 
         offsets = held.tile([P, N // 16], U16, name="offsets")
         nc.sync.dma_start(offsets[:], offs)

@@ -39,15 +39,18 @@ def tile_share_lstm_cell_kernel(tc, x, h_prev, c_prev, w_ih, w_hh, b_ih, b_hh, b
         w_ih_sb = held.tile([P, K_STEPS, GATES * H], BF16, name="w_ih_sb")
         h_sb = held.tile([P, K_STEPS, N], BF16, name="h_sb")
         w_hh_sb = held.tile([P, K_STEPS, GATES * H], BF16, name="w_hh_sb")
-        nc.sync.dma_start(x_sb[:], x.rearrange("(p k) n -> p k n", k=K_STEPS))
-        nc.sync.dma_start(w_ih_sb[:], w_ih.rearrange("(p k) m -> p k m", k=K_STEPS))
+        x_steps = x.rearrange("(p k) n -> k p n", k=K_STEPS)
+        w_ih_steps = w_ih.rearrange("(p k) m -> k p m", k=K_STEPS)
+        for k in range(K_STEPS):
+            nc.sync.dma_start(x_sb[:, k, :], x_steps[k])
+            nc.sync.dma_start(w_ih_sb[:, k, :], w_ih_steps[k])
         nc.sync.dma_start(h_sb[:], h_prev.rearrange("(p k) n -> p k n", k=K_STEPS))
         nc.sync.dma_start(w_hh_sb[:], w_hh.rearrange("(p k) m -> p k m", k=K_STEPS))
 
         b_ih_sb = held.tile([P, GATES, HALVES], F32, name="b_ih_sb")
         b_hh_sb = held.tile([P, GATES, HALVES], F32, name="b_hh_sb")
-        nc.scalar.dma_start(b_ih_sb[:], b_ih.rearrange("(g p half) o -> p g (half o)", g=GATES, half=HALVES))
-        nc.scalar.dma_start(b_hh_sb[:], b_hh.rearrange("(g p half) o -> p g (half o)", g=GATES, half=HALVES))
+        nc.sync.dma_start(b_ih_sb[:], b_ih.rearrange("(g p half) o -> p g (half o)", g=GATES, half=HALVES))
+        nc.sync.dma_start(b_hh_sb[:], b_hh.rearrange("(g p half) o -> p g (half o)", g=GATES, half=HALVES))
 
         offsets = held.tile([P, N // 16], U16, name="offsets")
         nc.sync.dma_start(offsets[:], offs)

@@ -14,6 +14,7 @@ HALVES = H // P
 GATES = 4
 GATE_I, GATE_F, GATE_O, GATE_CAND = 0, 1, 2, 3
 WARM_MATMULS = 4
+LAST_PIECES = 2
 
 FLOPS = 2 * (D + H) * GATES * H * N
 
@@ -23,7 +24,7 @@ def tile_share_lstm_cell_kernel(tc, x, h_prev, c_prev, w_ih, w_hh, b_ih, b_hh, b
     with (
         tc.tile_pool(name="held", bufs=1) as held,
         tc.tile_pool(name="work", bufs=2) as work,
-        tc.psum_pool(name="z_banks", bufs=6) as z_banks,
+        tc.psum_pool(name="z_banks", bufs=4) as z_banks,
         tc.psum_pool(name="warm_bank", bufs=1) as warm_bank,
     ):
         zeros = held.tile([P, N], BF16, name="zeros")
@@ -69,38 +70,47 @@ def tile_share_lstm_cell_kernel(tc, x, h_prev, c_prev, w_ih, w_hh, b_ih, b_hh, b
 
         steps = [(w_ih_sb, x_sb, k) for k in range(K_STEPS)] + [(w_hh_sb, h_sb, k) for k in range(K_STEPS)]
 
-        def gate_of(gate, half):
-            z = z_banks.tile([P, N], F32, name="z")
-            for step, (weights, moving, k) in enumerate(steps):
-                nc.tensor.matmul(
-                    z[:],
-                    weights[:, k, gate * H + half : (gate + 1) * H : HALVES],
-                    moving[:, k, :],
-                    start=(step == 0),
-                    stop=(step == len(steps) - 1),
-                )
+        def gate_of(gate, half, pieces=1):
             gate_tile = work.tile([P, N], F32, name=f"gate{gate}")
-            nc.scalar.activation(
-                gate_tile[:], z[:], TANH if gate == GATE_CAND else SIGMOID, bias=bias[:, gate, half : half + 1]
-            )
+            for columns in pieces_of(pieces):
+                z = z_banks.tile([P, N // pieces], F32, name="z")
+                for step, (weights, moving, k) in enumerate(steps):
+                    nc.tensor.matmul(
+                        z[:],
+                        weights[:, k, gate * H + half : (gate + 1) * H : HALVES],
+                        moving[:, k, columns],
+                        start=(step == 0),
+                        stop=(step == len(steps) - 1),
+                    )
+                nc.scalar.activation(
+                    gate_tile[:, columns],
+                    z[:],
+                    TANH if gate == GATE_CAND else SIGMOID,
+                    bias=bias[:, gate, half : half + 1],
+                )
             return gate_tile
+
+        def pieces_of(pieces):
+            return [slice(piece * (N // pieces), (piece + 1) * (N // pieces)) for piece in range(pieces)]
 
         tanh_cells = []
         for half in range(HALVES):
+            pieces = LAST_PIECES if half == HALVES - 1 else 1
             gate_i = gate_of(GATE_I, half)
             gate_cand = gate_of(GATE_CAND, half)
             written = work.tile([P, N], F32, name="written")
             nc.vector.tensor_tensor(written[:], gate_i[:], gate_cand[:], MULT)
-            gate_f = gate_of(GATE_F, half)
+            gate_f = gate_of(GATE_F, half, pieces)
             kept = work.tile([P, N], F32, name="kept")
-            nc.vector.tensor_tensor(kept[:], gate_f[:], c_sb[:, half, :], MULT)
             cell = work.tile([P, N], F32, name="cell")
-            nc.vector.tensor_tensor(cell[:], kept[:], written[:], ADD)
+            for columns in pieces_of(pieces):
+                nc.vector.tensor_tensor(kept[:, columns], gate_f[:, columns], c_sb[:, half, columns], MULT)
+                nc.vector.tensor_tensor(cell[:, columns], kept[:, columns], written[:, columns], ADD)
             tanh_cell = work.tile([P, N], F32, name="tanh_cell")
             nc.scalar.activation(tanh_cell[:], cell[:], TANH)
             tanh_cells.append(tanh_cell)
 
         for half in range(HALVES):
-            gate_o = gate_of(GATE_O, half)
+            gate_o = gate_of(GATE_O, half, LAST_PIECES if half == 0 else 1)
             nc.vector.tensor_tensor(windows[half][:].indirect(offsets[:]), gate_o[:], tanh_cells[half][:], MULT)
             nc.sync.dma_start(out_halves[half], windows[half][:])

@@ -14,6 +14,7 @@ HALVES = H // P
 GATES = 4
 GATE_I, GATE_F, GATE_O, GATE_CAND = 0, 1, 2, 3
 WARM_MATMULS = 4
+BLOCK = 8
 LAST_PIECES = 2
 
 FLOPS = 2 * (D + H) * GATES * H * N
@@ -48,10 +49,10 @@ def tile_share_lstm_cell_kernel(tc, x, h_prev, c_prev, w_ih, w_hh, b_ih, b_hh, b
         nc.sync.dma_start(h_sb[:], h_prev.rearrange("(p k) n -> p k n", k=K_STEPS))
         nc.sync.dma_start(w_hh_sb[:], w_hh.rearrange("(p k) m -> p k m", k=K_STEPS))
 
-        b_ih_sb = held.tile([P, GATES, HALVES], F32, name="b_ih_sb")
-        b_hh_sb = held.tile([P, GATES, HALVES], F32, name="b_hh_sb")
-        nc.sync.dma_start(b_ih_sb[:], b_ih.rearrange("(g p half) o -> p g (half o)", g=GATES, half=HALVES))
-        nc.sync.dma_start(b_hh_sb[:], b_hh.rearrange("(g p half) o -> p g (half o)", g=GATES, half=HALVES))
+        b_ih_sb = held.tile([P, GATES, BLOCK], F32, name="b_ih_sb")
+        b_hh_sb = held.tile([P, GATES, BLOCK], F32, name="b_hh_sb")
+        nc.sync.dma_start(b_ih_sb[:, :, 0:HALVES], b_ih.rearrange("(g p half) o -> p g (half o)", g=GATES, half=HALVES))
+        nc.sync.dma_start(b_hh_sb[:, :, 0:HALVES], b_hh.rearrange("(g p half) o -> p g (half o)", g=GATES, half=HALVES))
 
         offsets = held.tile([P, N // 16], U16, name="offsets")
         nc.sync.dma_start(offsets[:], offs)
@@ -66,7 +67,7 @@ def tile_share_lstm_cell_kernel(tc, x, h_prev, c_prev, w_ih, w_hh, b_ih, b_hh, b
             nc.sync.dma_start(windows[half][:], base_halves[half])
 
         bias = held.tile([P, GATES, HALVES], F32, name="bias")
-        nc.vector.tensor_tensor(bias[:], b_ih_sb[:], b_hh_sb[:], ADD)
+        nc.vector.tensor_tensor(bias[:], b_ih_sb[:, :, 0:HALVES], b_hh_sb[:, :, 0:HALVES], ADD)
 
         steps = [(w_ih_sb, x_sb, k) for k in range(K_STEPS)] + [(w_hh_sb, h_sb, k) for k in range(K_STEPS)]
 

@@ -2,7 +2,7 @@ import concourse.mybir as mybir
 
 BF16, F32, U16 = mybir.dt.bfloat16, mybir.dt.float32, mybir.dt.uint16
 SIGMOID, TANH = mybir.ActivationFunctionType.Sigmoid, mybir.ActivationFunctionType.Tanh
-MULT, ADD = mybir.AluOpType.mult, mybir.AluOpType.add
+MULT, ADD, IS_EQUAL = mybir.AluOpType.mult, mybir.AluOpType.add, mybir.AluOpType.is_equal
 
 P = 128
 D = 256
@@ -14,7 +14,10 @@ HALVES = H // P
 GATES = 4
 GATE_I, GATE_F, GATE_O, GATE_CAND = 0, 1, 2, 3
 WARM_MATMULS = 4
-BLOCK = 8
+ROWS = GATES * HALVES
+ROW_TILE = 32
+HH_ROW = ROW_TILE - ROWS
+IH_ROW = HH_ROW - ROWS
 LAST_PIECES = 2
 
 FLOPS = 2 * (D + H) * GATES * H * N
@@ -26,13 +29,29 @@ def tile_share_lstm_cell_kernel(tc, x, h_prev, c_prev, w_ih, w_hh, b_ih, b_hh, b
         tc.tile_pool(name="held", bufs=1) as held,
         tc.tile_pool(name="work", bufs=2) as work,
         tc.psum_pool(name="z_banks", bufs=4) as z_banks,
-        tc.psum_pool(name="warm_bank", bufs=1) as warm_bank,
+        tc.psum_pool(name="one_bank", bufs=1) as one_bank,
     ):
         zeros = held.tile([P, N], BF16, name="zeros")
         nc.vector.memset(zeros[:], 0.0)
-        warm_ps = warm_bank.tile([P, N], F32, name="warm_ps")
+        warm_ps = one_bank.tile([P, N], F32, name="warm_ps")
         for repeat in range(WARM_MATMULS):
             nc.tensor.matmul(warm_ps[:], zeros[:, :P], zeros[:], start=True, stop=True)
+
+        bias_rows = held.tile([ROW_TILE, P], F32, name="bias_rows")
+        nc.vector.memset(bias_rows[:IH_ROW, :], 0.0)
+        ones = held.tile([P, ROW_TILE], F32, name="ones")
+        column_number = held.tile([P, ROW_TILE], F32, name="column_number", align_bytes=64)
+        row_number = held.tile([P, ROW_TILE], F32, name="row_number", align_bytes=64)
+        nc.vector.memset(ones[:], 1.0)
+        nc.vector.tensor_tensor_scan(column_number[:], ones[:], ones[:], 0.0, MULT, ADD)
+        nc.vector.transpose(row_number[:], column_number[:])
+        picks = [held.tile([ROW_TILE, ROWS], F32, name=f"picks{vector}") for vector in range(2)]
+        for pick, first_row in zip(picks, (IH_ROW, HH_ROW)):
+            nc.vector.tensor_tensor(
+                pick[:], row_number[:ROW_TILE, 0:ROWS], column_number[:ROW_TILE, first_row : first_row + ROWS], IS_EQUAL
+            )
+        pick_rows = held.tile([ROW_TILE, ROWS], F32, name="pick_rows")
+        nc.vector.tensor_tensor(pick_rows[:], picks[0][:], picks[1][:], ADD)
 
         table_warm = held.tile([P, 1], F32, name="table_warm")
         nc.scalar.activation(table_warm[:], zeros[:, 0:1], SIGMOID)
@@ -46,28 +65,27 @@ def tile_share_lstm_cell_kernel(tc, x, h_prev, c_prev, w_ih, w_hh, b_ih, b_hh, b
         for k in range(K_STEPS):
             nc.sync.dma_start(x_sb[:, k, :], x_steps[k])
             nc.sync.dma_start(w_ih_sb[:, k, :], w_ih_steps[k])
+        nc.sync.dma_start(bias_rows[IH_ROW : IH_ROW + ROWS, :], b_ih.rearrange("(row p) o -> row (p o)", p=P))
+        nc.sync.dma_start(bias_rows[HH_ROW : HH_ROW + ROWS, :], b_hh.rearrange("(row p) o -> row (p o)", p=P))
         nc.sync.dma_start(h_sb[:], h_prev.rearrange("(p k) n -> p k n", k=K_STEPS))
         nc.sync.dma_start(w_hh_sb[:], w_hh.rearrange("(p k) m -> p k m", k=K_STEPS))
-
-        b_ih_sb = held.tile([P, GATES, BLOCK], F32, name="b_ih_sb")
-        b_hh_sb = held.tile([P, GATES, BLOCK], F32, name="b_hh_sb")
-        nc.sync.dma_start(b_ih_sb[:, :, 0:HALVES], b_ih.rearrange("(g p half) o -> p g (half o)", g=GATES, half=HALVES))
-        nc.sync.dma_start(b_hh_sb[:, :, 0:HALVES], b_hh.rearrange("(g p half) o -> p g (half o)", g=GATES, half=HALVES))
 
         offsets = held.tile([P, N // 16], U16, name="offsets")
         nc.sync.dma_start(offsets[:], offs)
 
         c_sb = held.tile([P, HALVES, N], F32, name="c_sb")
-        nc.sync.dma_start(c_sb[:], c_prev.rearrange("(p half) n -> p half n", half=HALVES))
+        nc.sync.dma_start(c_sb[:], c_prev.rearrange("(half p) n -> p half n", half=HALVES))
 
-        base_halves = base.rearrange("(p half) s -> half p s", half=HALVES)
-        out_halves = out.rearrange("(p half) s -> half p s", half=HALVES)
+        base_halves = base.rearrange("(half p) s -> half p s", half=HALVES)
+        out_halves = out.rearrange("(half p) s -> half p s", half=HALVES)
         windows = [held.tile([P, S], F32, name=f"window{half}") for half in range(HALVES)]
         for half in range(HALVES):
             nc.sync.dma_start(windows[half][:], base_halves[half])
 
-        bias = held.tile([P, GATES, HALVES], F32, name="bias")
-        nc.vector.tensor_tensor(bias[:], b_ih_sb[:, :, 0:HALVES], b_hh_sb[:, :, 0:HALVES], ADD)
+        turned = one_bank.tile([P, ROWS], F32, name="turned")
+        nc.tensor.matmul(turned[:], bias_rows[:], pick_rows[:], start=True, stop=True)
+        bias = held.tile([P, ROWS], F32, name="bias")
+        nc.vector.tensor_copy(bias[:], turned[:])
 
         steps = [(w_ih_sb, x_sb, k) for k in range(K_STEPS)] + [(w_hh_sb, h_sb, k) for k in range(K_STEPS)]
 
@@ -75,10 +93,11 @@ def tile_share_lstm_cell_kernel(tc, x, h_prev, c_prev, w_ih, w_hh, b_ih, b_hh, b
             gate_tile = work.tile([P, N], F32, name=f"gate{gate}")
             for columns in pieces_of(pieces):
                 z = z_banks.tile([P, N // pieces], F32, name="z")
+                row = gate * HALVES + half
                 for step, (weights, moving, k) in enumerate(steps):
                     nc.tensor.matmul(
                         z[:],
-                        weights[:, k, gate * H + half : (gate + 1) * H : HALVES],
+                        weights[:, k, row * P : (row + 1) * P],
                         moving[:, k, columns],
                         start=(step == 0),
                         stop=(step == len(steps) - 1),
@@ -87,7 +106,7 @@ def tile_share_lstm_cell_kernel(tc, x, h_prev, c_prev, w_ih, w_hh, b_ih, b_hh, b
                     gate_tile[:, columns],
                     z[:],
                     TANH if gate == GATE_CAND else SIGMOID,
-                    bias=bias[:, gate, half : half + 1],
+                    bias=bias[:, row : row + 1],
                 )
             return gate_tile
 

@@ -13,12 +13,12 @@ K_STEPS = D // P
 HALVES = H // P
 GATES = 4
 GATE_I, GATE_F, GATE_O, GATE_CAND = 0, 1, 2, 3
-WARM_MATMULS = 4
+WARM_MATMULS = 12
 ROWS = GATES * HALVES
 ROW_TILE = 32
 HH_ROW = ROW_TILE - ROWS
 IH_ROW = HH_ROW - ROWS
-LAST_PIECES = 2
+AHEAD = 5
 
 FLOPS = 2 * (D + H) * GATES * H * N
 
@@ -27,17 +27,18 @@ def tile_share_lstm_cell_kernel(tc, x, h_prev, c_prev, w_ih, w_hh, b_ih, b_hh, b
     nc = tc.nc
     with (
         tc.tile_pool(name="held", bufs=1) as held,
-        tc.tile_pool(name="work", bufs=2) as work,
-        tc.psum_pool(name="z_banks", bufs=4) as z_banks,
+        tc.psum_pool(name="z_banks", bufs=5) as z_banks,
         tc.psum_pool(name="one_bank", bufs=1) as one_bank,
     ):
-        zeros = held.tile([P, N], BF16, name="zeros")
+        zeros = held.tile([P, P], BF16, name="zeros")
         nc.vector.memset(zeros[:], 0.0)
-        warm_ps = one_bank.tile([P, N], F32, name="warm_ps")
+        warm_ps = one_bank.tile([P, P], F32, name="warm_ps")
         for repeat in range(WARM_MATMULS):
-            nc.tensor.matmul(warm_ps[:], zeros[:, :P], zeros[:], start=True, stop=True)
+            nc.tensor.matmul(warm_ps[:], zeros[:], zeros[:], start=True, stop=True)
 
         bias_rows = held.tile([ROW_TILE, P], F32, name="bias_rows")
+        nc.sync.dma_start(bias_rows[IH_ROW : IH_ROW + ROWS, :], b_ih.rearrange("(row p) o -> row (p o)", p=P))
+        nc.sync.dma_start(bias_rows[HH_ROW : HH_ROW + ROWS, :], b_hh.rearrange("(row p) o -> row (p o)", p=P))
         nc.vector.memset(bias_rows[:IH_ROW, :], 0.0)
         ones = held.tile([P, ROW_TILE], F32, name="ones")
         column_number = held.tile([P, ROW_TILE], F32, name="column_number", align_bytes=64)
@@ -53,6 +54,11 @@ def tile_share_lstm_cell_kernel(tc, x, h_prev, c_prev, w_ih, w_hh, b_ih, b_hh, b
         pick_rows = held.tile([ROW_TILE, ROWS], F32, name="pick_rows")
         nc.vector.tensor_tensor(pick_rows[:], picks[0][:], picks[1][:], ADD)
 
+        turned = one_bank.tile([P, ROWS], F32, name="turned")
+        nc.tensor.matmul(turned[:], bias_rows[:], pick_rows[:], start=True, stop=True)
+        bias = held.tile([P, ROWS], F32, name="bias")
+        nc.vector.tensor_copy(bias[:], turned[:])
+
         table_warm = held.tile([P, 1], F32, name="table_warm")
         nc.scalar.activation(table_warm[:], zeros[:, 0:1], SIGMOID)
 
@@ -64,9 +70,8 @@ def tile_share_lstm_cell_kernel(tc, x, h_prev, c_prev, w_ih, w_hh, b_ih, b_hh, b
         w_ih_steps = w_ih.rearrange("(p k) m -> k p m", k=K_STEPS)
         for k in range(K_STEPS):
             nc.sync.dma_start(x_sb[:, k, :], x_steps[k])
-            nc.sync.dma_start(w_ih_sb[:, k, :], w_ih_steps[k])
-        nc.sync.dma_start(bias_rows[IH_ROW : IH_ROW + ROWS, :], b_ih.rearrange("(row p) o -> row (p o)", p=P))
-        nc.sync.dma_start(bias_rows[HH_ROW : HH_ROW + ROWS, :], b_hh.rearrange("(row p) o -> row (p o)", p=P))
+            for gates_columns in (slice(0, H), slice(H, GATES * H)) if k == 0 else (slice(0, GATES * H),):
+                nc.sync.dma_start(w_ih_sb[:, k, gates_columns], w_ih_steps[k][:, gates_columns])
         nc.sync.dma_start(h_sb[:], h_prev.rearrange("(p k) n -> p k n", k=K_STEPS))
         nc.sync.dma_start(w_hh_sb[:], w_hh.rearrange("(p k) m -> p k m", k=K_STEPS))
 
@@ -82,55 +87,62 @@ def tile_share_lstm_cell_kernel(tc, x, h_prev, c_prev, w_ih, w_hh, b_ih, b_hh, b
         for half in range(HALVES):
             nc.sync.dma_start(windows[half][:], base_halves[half])
 
-        turned = one_bank.tile([P, ROWS], F32, name="turned")
-        nc.tensor.matmul(turned[:], bias_rows[:], pick_rows[:], start=True, stop=True)
-        bias = held.tile([P, ROWS], F32, name="bias")
-        nc.vector.tensor_copy(bias[:], turned[:])
-
         steps = [(w_ih_sb, x_sb, k) for k in range(K_STEPS)] + [(w_hh_sb, h_sb, k) for k in range(K_STEPS)]
 
-        def gate_of(gate, half, pieces=1):
-            gate_tile = work.tile([P, N], F32, name=f"gate{gate}")
-            for columns in pieces_of(pieces):
-                z = z_banks.tile([P, N // pieces], F32, name="z")
-                row = gate * HALVES + half
-                for step, (weights, moving, k) in enumerate(steps):
-                    nc.tensor.matmul(
-                        z[:],
-                        weights[:, k, row * P : (row + 1) * P],
-                        moving[:, k, columns],
-                        start=(step == 0),
-                        stop=(step == len(steps) - 1),
-                    )
-                nc.scalar.activation(
-                    gate_tile[:, columns],
+        def bank_for(gate, half, columns):
+            return z_banks.tile([P, columns.stop - columns.start], F32, name="z")
+
+        def multiply(z, gate, half, columns, first, last):
+            row = gate * HALVES + half
+            for step in range(first, last):
+                weights, moving, k = steps[step]
+                nc.tensor.matmul(
                     z[:],
-                    TANH if gate == GATE_CAND else SIGMOID,
-                    bias=bias[:, row : row + 1],
+                    weights[:, k, row * P : (row + 1) * P],
+                    moving[:, k, columns],
+                    start=(step == 0),
+                    stop=(step == len(steps) - 1),
                 )
-            return gate_tile
 
-        def pieces_of(pieces):
-            return [slice(piece * (N // pieces), (piece + 1) * (N // pieces)) for piece in range(pieces)]
+        def activate(z, gate, half, columns, gate_tile):
+            row = gate * HALVES + half
+            nc.scalar.activation(
+                gate_tile[:, columns], z[:], TANH if gate == GATE_CAND else SIGMOID, bias=bias[:, row : row + 1]
+            )
 
-        tanh_cells = []
-        for half in range(HALVES):
-            pieces = LAST_PIECES if half == HALVES - 1 else 1
-            gate_i = gate_of(GATE_I, half)
-            gate_cand = gate_of(GATE_CAND, half)
-            written = work.tile([P, N], F32, name="written")
-            nc.vector.tensor_tensor(written[:], gate_i[:], gate_cand[:], MULT)
-            gate_f = gate_of(GATE_F, half, pieces)
-            kept = work.tile([P, N], F32, name="kept")
-            cell = work.tile([P, N], F32, name="cell")
-            for columns in pieces_of(pieces):
-                nc.vector.tensor_tensor(kept[:, columns], gate_f[:, columns], c_sb[:, half, columns], MULT)
-                nc.vector.tensor_tensor(cell[:, columns], kept[:, columns], written[:, columns], ADD)
-            tanh_cell = work.tile([P, N], F32, name="tanh_cell")
-            nc.scalar.activation(tanh_cell[:], cell[:], TANH)
-            tanh_cells.append(tanh_cell)
+        whole = slice(0, N)
+        pieces = [slice(0, N // 2), slice(N // 2, N)]
+        order = [(gate, half, whole) for half in range(HALVES) for gate in (GATE_I, GATE_CAND, GATE_F)]
+        order = order[:-1] + [(GATE_F, 1, piece) for piece in pieces]
+        order += [(GATE_O, 0, piece) for piece in pieces] + [(GATE_O, 1, whole)]
 
-        for half in range(HALVES):
-            gate_o = gate_of(GATE_O, half, LAST_PIECES if half == 0 else 1)
-            nc.vector.tensor_tensor(windows[half][:].indirect(offsets[:]), gate_o[:], tanh_cells[half][:], MULT)
-            nc.sync.dma_start(out_halves[half], windows[half][:])
+        ahead = [bank_for(*product) for product in order[:AHEAD]]
+        for k in range(K_STEPS):
+            for z, product in zip(ahead, order):
+                multiply(z, *product, k, k + 1)
+
+        gates = {}
+        cells = [held.tile([P, N], F32, name=f"cell{half}") for half in range(HALVES)]
+        writtens = [held.tile([P, N], F32, name=f"written{half}") for half in range(HALVES)]
+        kepts = [held.tile([P, N], F32, name=f"kept{half}") for half in range(HALVES)]
+        tanh_cells = [held.tile([P, N], F32, name=f"tanh_cell{half}") for half in range(HALVES)]
+        for gate in range(GATES):
+            for half in range(HALVES):
+                gates[gate, half] = held.tile([P, N], F32, name=f"gate{gate}_{half}")
+        for at, (gate, half, columns) in enumerate(order):
+            z = ahead[at] if at < AHEAD else bank_for(gate, half, columns)
+            multiply(z, gate, half, columns, K_STEPS if at < AHEAD else 0, len(steps))
+            activate(z, gate, half, columns, gates[gate, half])
+            if gate == GATE_CAND:
+                nc.vector.tensor_tensor(writtens[half][:], gates[GATE_I, half][:], gates[GATE_CAND, half][:], MULT)
+            if gate == GATE_F:
+                kept, cell = kepts[half][:, columns], cells[half][:, columns]
+                nc.vector.tensor_tensor(kept, gates[GATE_F, half][:, columns], c_sb[:, half, columns], MULT)
+                nc.vector.tensor_tensor(cell, kept, writtens[half][:, columns], ADD)
+                if columns.stop == N:
+                    nc.scalar.activation(tanh_cells[half][:], cells[half][:], TANH)
+            if gate == GATE_O and columns.stop == N:
+                nc.vector.tensor_tensor(
+                    windows[half][:].indirect(offsets[:]), gates[GATE_O, half][:], tanh_cells[half][:], MULT
+                )
+                nc.sync.dma_start(out_halves[half], windows[half][:])

@@ -13,7 +13,7 @@ K_STEPS = D // P
 HALVES = H // P
 GATES = 4
 GATE_I, GATE_F, GATE_O, GATE_CAND = 0, 1, 2, 3
-WARM_MATMULS = 12
+WARM_MATMULS = 17
 ROWS = GATES * HALVES
 ROW_TILE = 32
 HH_ROW = ROW_TILE - ROWS
@@ -70,8 +70,7 @@ def tile_share_lstm_cell_kernel(tc, x, h_prev, c_prev, w_ih, w_hh, b_ih, b_hh, b
         w_ih_steps = w_ih.rearrange("(p k) m -> k p m", k=K_STEPS)
         for k in range(K_STEPS):
             nc.sync.dma_start(x_sb[:, k, :], x_steps[k])
-            for gates_columns in (slice(0, H), slice(H, GATES * H)) if k == 0 else (slice(0, GATES * H),):
-                nc.sync.dma_start(w_ih_sb[:, k, gates_columns], w_ih_steps[k][:, gates_columns])
+            nc.sync.dma_start(w_ih_sb[:, k, :], w_ih_steps[k])
         nc.sync.dma_start(h_sb[:], h_prev.rearrange("(p k) n -> p k n", k=K_STEPS))
         nc.sync.dma_start(w_hh_sb[:], w_hh.rearrange("(p k) m -> p k m", k=K_STEPS))
 

@@ -13,7 +13,7 @@ K_STEPS = D // P
 HALVES = H // P
 GATES = 4
 GATE_I, GATE_F, GATE_O, GATE_CAND = 0, 1, 2, 3
-WARM_MATMULS = 17
+WARM_MATMULS = 14
 ROWS = GATES * HALVES
 ROW_TILE = 32
 HH_ROW = ROW_TILE - ROWS
@@ -37,8 +37,6 @@ def tile_share_lstm_cell_kernel(tc, x, h_prev, c_prev, w_ih, w_hh, b_ih, b_hh, b
             nc.tensor.matmul(warm_ps[:], zeros[:], zeros[:], start=True, stop=True)
 
         bias_rows = held.tile([ROW_TILE, P], F32, name="bias_rows")
-        nc.sync.dma_start(bias_rows[IH_ROW : IH_ROW + ROWS, :], b_ih.rearrange("(row p) o -> row (p o)", p=P))
-        nc.sync.dma_start(bias_rows[HH_ROW : HH_ROW + ROWS, :], b_hh.rearrange("(row p) o -> row (p o)", p=P))
         nc.vector.memset(bias_rows[:IH_ROW, :], 0.0)
         ones = held.tile([P, ROW_TILE], F32, name="ones")
         column_number = held.tile([P, ROW_TILE], F32, name="column_number", align_bytes=64)
@@ -54,11 +52,6 @@ def tile_share_lstm_cell_kernel(tc, x, h_prev, c_prev, w_ih, w_hh, b_ih, b_hh, b
         pick_rows = held.tile([ROW_TILE, ROWS], F32, name="pick_rows")
         nc.vector.tensor_tensor(pick_rows[:], picks[0][:], picks[1][:], ADD)
 
-        turned = one_bank.tile([P, ROWS], F32, name="turned")
-        nc.tensor.matmul(turned[:], bias_rows[:], pick_rows[:], start=True, stop=True)
-        bias = held.tile([P, ROWS], F32, name="bias")
-        nc.vector.tensor_copy(bias[:], turned[:])
-
         table_warm = held.tile([P, 1], F32, name="table_warm")
         nc.scalar.activation(table_warm[:], zeros[:, 0:1], SIGMOID)
 
@@ -70,6 +63,9 @@ def tile_share_lstm_cell_kernel(tc, x, h_prev, c_prev, w_ih, w_hh, b_ih, b_hh, b
         w_ih_steps = w_ih.rearrange("(p k) m -> k p m", k=K_STEPS)
         for k in range(K_STEPS):
             nc.sync.dma_start(x_sb[:, k, :], x_steps[k])
+            if k == 0:
+                nc.sync.dma_start(bias_rows[IH_ROW : IH_ROW + ROWS, :], b_ih.rearrange("(row p) o -> row (p o)", p=P))
+                nc.sync.dma_start(bias_rows[HH_ROW : HH_ROW + ROWS, :], b_hh.rearrange("(row p) o -> row (p o)", p=P))
             nc.sync.dma_start(w_ih_sb[:, k, :], w_ih_steps[k])
         nc.sync.dma_start(h_sb[:], h_prev.rearrange("(p k) n -> p k n", k=K_STEPS))
         nc.sync.dma_start(w_hh_sb[:], w_hh.rearrange("(p k) m -> p k m", k=K_STEPS))
@@ -114,6 +110,11 @@ def tile_share_lstm_cell_kernel(tc, x, h_prev, c_prev, w_ih, w_hh, b_ih, b_hh, b
         order = [(gate, half, whole) for half in range(HALVES) for gate in (GATE_I, GATE_CAND, GATE_F)]
         order = order[:-1] + [(GATE_F, 1, piece) for piece in pieces]
         order += [(GATE_O, 0, piece) for piece in pieces] + [(GATE_O, 1, whole)]
+
+        turned = one_bank.tile([P, ROWS], F32, name="turned")
+        nc.tensor.matmul(turned[:], bias_rows[:], pick_rows[:], start=True, stop=True)
+        bias = held.tile([P, ROWS], F32, name="bias")
+        nc.vector.tensor_copy(bias[:], turned[:])
 
         ahead = [bank_for(*product) for product in order[:AHEAD]]
         for k in range(K_STEPS):

@@ -13,7 +13,7 @@ K_STEPS = D // P
 HALVES = H // P
 GATES = 4
 GATE_I, GATE_F, GATE_O, GATE_CAND = 0, 1, 2, 3
-WARM_MATMULS = 14
+WARM_MATMULS = 12
 ROWS = GATES * HALVES
 ROW_TILE = 32
 HH_ROW = ROW_TILE - ROWS
@@ -66,7 +66,8 @@ def tile_share_lstm_cell_kernel(tc, x, h_prev, c_prev, w_ih, w_hh, b_ih, b_hh, b
             if k == 0:
                 nc.sync.dma_start(bias_rows[IH_ROW : IH_ROW + ROWS, :], b_ih.rearrange("(row p) o -> row (p o)", p=P))
                 nc.sync.dma_start(bias_rows[HH_ROW : HH_ROW + ROWS, :], b_hh.rearrange("(row p) o -> row (p o)", p=P))
-            nc.sync.dma_start(w_ih_sb[:, k, :], w_ih_steps[k])
+            for gate_columns in (slice(0, H), slice(H, GATES * H)) if k == 0 else (slice(0, GATES * H),):
+                nc.sync.dma_start(w_ih_sb[:, k, gate_columns], w_ih_steps[k][:, gate_columns])
         nc.sync.dma_start(h_sb[:], h_prev.rearrange("(p k) n -> p k n", k=K_STEPS))
         nc.sync.dma_start(w_hh_sb[:], w_hh.rearrange("(p k) m -> p k m", k=K_STEPS))
 

@@ -13,7 +13,7 @@ K_STEPS = D // P
 HALVES = H // P
 GATES = 4
 GATE_I, GATE_F, GATE_O, GATE_CAND = 0, 1, 2, 3
-WARM_MATMULS = 12
+WARM_MATMULS = 14
 ROWS = GATES * HALVES
 ROW_TILE = 32
 HH_ROW = ROW_TILE - ROWS

import concourse.mybir as mybir

BF16, F32, U16 = mybir.dt.bfloat16, mybir.dt.float32, mybir.dt.uint16
SIGMOID, TANH = mybir.ActivationFunctionType.Sigmoid, mybir.ActivationFunctionType.Tanh
MULT, ADD, IS_EQUAL = mybir.AluOpType.mult, mybir.AluOpType.add, mybir.AluOpType.is_equal

P = 128
D = 256
H = 256
N = 512
S = 4096
K_STEPS = D // P
HALVES = H // P
GATES = 4
GATE_I, GATE_F, GATE_O, GATE_CAND = 0, 1, 2, 3
WARM_MATMULS = 14
ROWS = GATES * HALVES
ROW_TILE = 32
HH_ROW = ROW_TILE - ROWS
IH_ROW = HH_ROW - ROWS
AHEAD = 5

FLOPS = 2 * (D + H) * GATES * H * N


def tile_share_lstm_cell_kernel(tc, x, h_prev, c_prev, w_ih, w_hh, b_ih, b_hh, base, offs, out):
    nc = tc.nc
    with (
        tc.tile_pool(name="held", bufs=1) as held,
        tc.psum_pool(name="z_banks", bufs=5) as z_banks,
        tc.psum_pool(name="one_bank", bufs=1) as one_bank,
    ):
        zeros = held.tile([P, P], BF16, name="zeros")
        nc.vector.memset(zeros[:], 0.0)
        warm_ps = one_bank.tile([P, P], F32, name="warm_ps")
        for repeat in range(WARM_MATMULS):
            nc.tensor.matmul(warm_ps[:], zeros[:], zeros[:], start=True, stop=True)

        bias_rows = held.tile([ROW_TILE, P], F32, name="bias_rows")
        nc.vector.memset(bias_rows[:IH_ROW, :], 0.0)
        ones = held.tile([P, ROW_TILE], F32, name="ones")
        column_number = held.tile([P, ROW_TILE], F32, name="column_number", align_bytes=64)
        row_number = held.tile([P, ROW_TILE], F32, name="row_number", align_bytes=64)
        nc.vector.memset(ones[:], 1.0)
        nc.vector.tensor_tensor_scan(column_number[:], ones[:], ones[:], 0.0, MULT, ADD)
        nc.vector.transpose(row_number[:], column_number[:])
        picks = [held.tile([ROW_TILE, ROWS], F32, name=f"picks{vector}") for vector in range(2)]
        for pick, first_row in zip(picks, (IH_ROW, HH_ROW)):
            nc.vector.tensor_tensor(
                pick[:], row_number[:ROW_TILE, 0:ROWS], column_number[:ROW_TILE, first_row : first_row + ROWS], IS_EQUAL
            )
        pick_rows = held.tile([ROW_TILE, ROWS], F32, name="pick_rows")
        nc.vector.tensor_tensor(pick_rows[:], picks[0][:], picks[1][:], ADD)

        table_warm = held.tile([P, 1], F32, name="table_warm")
        nc.scalar.activation(table_warm[:], zeros[:, 0:1], SIGMOID)

        x_sb = held.tile([P, K_STEPS, N], BF16, name="x_sb")
        w_ih_sb = held.tile([P, K_STEPS, GATES * H], BF16, name="w_ih_sb")
        h_sb = held.tile([P, K_STEPS, N], BF16, name="h_sb")
        w_hh_sb = held.tile([P, K_STEPS, GATES * H], BF16, name="w_hh_sb")
        x_steps = x.rearrange("(p k) n -> k p n", k=K_STEPS)
        w_ih_steps = w_ih.rearrange("(p k) m -> k p m", k=K_STEPS)
        for k in range(K_STEPS):
            nc.sync.dma_start(x_sb[:, k, :], x_steps[k])
            if k == 0:
                nc.sync.dma_start(bias_rows[IH_ROW : IH_ROW + ROWS, :], b_ih.rearrange("(row p) o -> row (p o)", p=P))
                nc.sync.dma_start(bias_rows[HH_ROW : HH_ROW + ROWS, :], b_hh.rearrange("(row p) o -> row (p o)", p=P))
            for gate_columns in (slice(0, H), slice(H, GATES * H)) if k == 0 else (slice(0, GATES * H),):
                nc.sync.dma_start(w_ih_sb[:, k, gate_columns], w_ih_steps[k][:, gate_columns])
        nc.sync.dma_start(h_sb[:], h_prev.rearrange("(p k) n -> p k n", k=K_STEPS))
        nc.sync.dma_start(w_hh_sb[:], w_hh.rearrange("(p k) m -> p k m", k=K_STEPS))

        offsets = held.tile([P, N // 16], U16, name="offsets")
        nc.sync.dma_start(offsets[:], offs)

        c_sb = held.tile([P, HALVES, N], F32, name="c_sb")
        nc.sync.dma_start(c_sb[:], c_prev.rearrange("(half p) n -> p half n", half=HALVES))

        base_halves = base.rearrange("(half p) s -> half p s", half=HALVES)
        out_halves = out.rearrange("(half p) s -> half p s", half=HALVES)
        windows = [held.tile([P, S], F32, name=f"window{half}") for half in range(HALVES)]
        for half in range(HALVES):
            nc.sync.dma_start(windows[half][:], base_halves[half])

        steps = [(w_ih_sb, x_sb, k) for k in range(K_STEPS)] + [(w_hh_sb, h_sb, k) for k in range(K_STEPS)]

        def bank_for(gate, half, columns):
            return z_banks.tile([P, columns.stop - columns.start], F32, name="z")

        def multiply(z, gate, half, columns, first, last):
            row = gate * HALVES + half
            for step in range(first, last):
                weights, moving, k = steps[step]
                nc.tensor.matmul(
                    z[:],
                    weights[:, k, row * P : (row + 1) * P],
                    moving[:, k, columns],
                    start=(step == 0),
                    stop=(step == len(steps) - 1),
                )

        def activate(z, gate, half, columns, gate_tile):
            row = gate * HALVES + half
            nc.scalar.activation(
                gate_tile[:, columns], z[:], TANH if gate == GATE_CAND else SIGMOID, bias=bias[:, row : row + 1]
            )

        whole = slice(0, N)
        pieces = [slice(0, N // 2), slice(N // 2, N)]
        order = [(gate, half, whole) for half in range(HALVES) for gate in (GATE_I, GATE_CAND, GATE_F)]
        order = order[:-1] + [(GATE_F, 1, piece) for piece in pieces]
        order += [(GATE_O, 0, piece) for piece in pieces] + [(GATE_O, 1, whole)]

        turned = one_bank.tile([P, ROWS], F32, name="turned")
        nc.tensor.matmul(turned[:], bias_rows[:], pick_rows[:], start=True, stop=True)
        bias = held.tile([P, ROWS], F32, name="bias")
        nc.vector.tensor_copy(bias[:], turned[:])

        ahead = [bank_for(*product) for product in order[:AHEAD]]
        for k in range(K_STEPS):
            for z, product in zip(ahead, order):
                multiply(z, *product, k, k + 1)

        gates = {}
        cells = [held.tile([P, N], F32, name=f"cell{half}") for half in range(HALVES)]
        writtens = [held.tile([P, N], F32, name=f"written{half}") for half in range(HALVES)]
        kepts = [held.tile([P, N], F32, name=f"kept{half}") for half in range(HALVES)]
        tanh_cells = [held.tile([P, N], F32, name=f"tanh_cell{half}") for half in range(HALVES)]
        for gate in range(GATES):
            for half in range(HALVES):
                gates[gate, half] = held.tile([P, N], F32, name=f"gate{gate}_{half}")
        for at, (gate, half, columns) in enumerate(order):
            z = ahead[at] if at < AHEAD else bank_for(gate, half, columns)
            multiply(z, gate, half, columns, K_STEPS if at < AHEAD else 0, len(steps))
            activate(z, gate, half, columns, gates[gate, half])
            if gate == GATE_CAND:
                nc.vector.tensor_tensor(writtens[half][:], gates[GATE_I, half][:], gates[GATE_CAND, half][:], MULT)
            if gate == GATE_F:
                kept, cell = kepts[half][:, columns], cells[half][:, columns]
                nc.vector.tensor_tensor(kept, gates[GATE_F, half][:, columns], c_sb[:, half, columns], MULT)
                nc.vector.tensor_tensor(cell, kept, writtens[half][:, columns], ADD)
                if columns.stop == N:
                    nc.scalar.activation(tanh_cells[half][:], cells[half][:], TANH)
            if gate == GATE_O and columns.stop == N:
                nc.vector.tensor_tensor(
                    windows[half][:].indirect(offsets[:]), gates[GATE_O, half][:], tanh_cells[half][:], MULT
                )
                nc.sync.dma_start(out_halves[half], windows[half][:])
